import numpy as np
import ml_dtypes


def mxq(x, axis, fmt="e4m3"):
    dtype, down = {"e4m3": (ml_dtypes.float8_e4m3fn, 7), "e5m2": (ml_dtypes.float8_e5m2, 14)}[fmt]
    v = np.moveaxis(np.asarray(x, np.float32).astype(ml_dtypes.bfloat16).astype(np.float64), axis, -1)
    blocks = v.reshape(v.shape[:-1] + (-1, 32))
    amax = np.abs(blocks).max(-1, keepdims=True)
    byte = np.maximum(np.where(amax > 0, np.frexp(amax)[1] - 1 + 127, 0) - down, 1)
    scale = np.exp2(byte - 127.0)
    codes = (blocks / scale).astype(np.float32).astype(dtype).astype(np.float64)
    return np.moveaxis((codes * scale).reshape(v.shape), -1, axis)


WIDE = False


def mx_kscale(k):
    if not WIDE:
        return np.ones(k)
    levels = np.array([10, -10, 5, -5, 0])
    if k % 512:
        return np.exp2(np.random.permutation(np.resize(levels, k // 32))).repeat(32)
    a = np.empty((k // 512, 16))
    for p in range(k // 512):
        a[p, :8] = np.random.permutation(np.resize(levels, 8))
        for g in range(8):
            far = levels[np.abs(levels - a[p, g]) >= 10]
            a[p, g + 8] = far[np.random.randint(len(far))]
    return np.exp2(a.ravel()).repeat(32)


BF16 = ml_dtypes.bfloat16


def bf(x):
    return np.asarray(x, np.float32).astype(BF16)


def f64(x):
    return np.asarray(x).astype(np.float64)


E2M1 = np.array([0.0, 0.5, 1.0, 1.5, 2.0, 3.0, 4.0, 6.0, -0.0, -0.5, -1.0, -1.5, -2.0, -3.0, -4.0, -6.0])


def pack_weight(w, fmt):
    k, n = w.shape
    w = f64(bf(w)).reshape(k // 32, 32, n)
    amax = np.abs(w).max(1)
    if fmt == "e4m3":
        byte = np.frexp(amax)[1] - 1 + 127 - 7
    else:
        mant, ex = np.frexp(amax / 6.0)
        byte = np.where(mant > 0.5, ex, ex - 1) + 127
    byte = np.clip(np.where(amax > 0, byte, 1), 1, 254)
    scaled = (w * np.exp2(127.0 - byte)[:, None, :]).reshape(k, n).astype(np.float32)
    by_word = np.ascontiguousarray(scaled.reshape(k // 512, 128, 4, n).transpose(0, 1, 3, 2))
    if fmt == "e4m3":
        words = by_word.astype(ml_dtypes.float8_e4m3fn).view(np.uint8)
    else:
        c = by_word.astype(ml_dtypes.float4_e2m1fn).view(np.uint8) & 0xF
        words = c[..., 0::2] | (c[..., 1::2] << 4)
    return np.ascontiguousarray(words), np.ascontiguousarray(byte.astype(np.uint8).reshape(k // 512, 16, n))


def unpack_weight(words, scales, fmt):
    g, p, n, _ = words.shape
    if fmt == "e4m3":
        vals = np.ascontiguousarray(words).view(ml_dtypes.float8_e4m3fn).astype(np.float64)
    else:
        nib = np.empty((g, p, n, 4), np.uint8)
        nib[..., 0::2] = words & 0xF
        nib[..., 1::2] = words >> 4
        vals = E2M1[nib]
    vals = vals * np.repeat(np.exp2(scales.astype(np.float64) - 127.0), 8, axis=1)[..., None]
    return vals.transpose(0, 1, 3, 2).reshape(g * 512, n)


M, N, NFEAT, NHID, NCLASS = 2048, 2048, 512, 512, 8
ADJ_P = 0.01
SIG = 4.5


def draw0():
    s = mx_kscale(NHID)
    t = mx_kscale(NHID)
    c = np.sqrt(2.0 * SIG / np.sqrt(NHID)) / np.sqrt(NHID)
    h = bf(np.maximum(np.random.standard_normal((N, NHID)), 0.0) * s[None, :])
    adj = bf(np.random.uniform(size=(N, N)) < ADJ_P)
    Qw_words, Qw_scales = pack_weight(np.random.standard_normal((NHID, NHID)) * c / s[:, None] * t[None, :], "e4m3")
    Qb = bf(np.random.standard_normal(NHID) * 0.1 * t)
    Kw_words, Kw_scales = pack_weight(np.random.standard_normal((NHID, NHID)) * c / s[:, None] / t[None, :], "e4m3")
    Kb = bf(np.random.standard_normal(NHID) * 0.1 / t)
    return {"h": h,
            "adj": adj,
            "Qw_words": Qw_words,
            "Qw_scales": Qw_scales,
            "Qb": Qb,
            "Kw_words": Kw_words,
            "Kw_scales": Kw_scales,
            "Kb": Kb}


def core(h, adj, Qw_words, Qw_scales, Qb, Kw_words, Kw_scales, Kb):
    hq = mxq(f64(h), 1, "e4m3")
    q = (hq @ unpack_weight(Qw_words, Qw_scales, "e4m3")) + f64(Qb)
    k = (hq @ unpack_weight(Kw_words, Kw_scales, "e4m3")) + f64(Kb)
    sc = f64(adj) * (mxq(q, 1, "e4m3") @ mxq(k, 1, "e4m3").T)
    e = np.exp(sc - sc.max(axis=1, keepdims=True))
    return e / e.sum(axis=1, keepdims=True)


def e4m3fn_bytes(y):
    return np.clip(np.asarray(y, np.float64), -448.0, 448.0).astype(np.float32).astype(ml_dtypes.float8_e4m3fn).view(np.uint8)


def e4m3fn_values(b):
    return np.asarray(b, np.uint8).view(ml_dtypes.float8_e4m3fn).astype(np.float64)


def setup_inputs():
    d = draw0()
    x0 = np.asarray(d['h']).astype(np.float64)
    s = (np.max(np.abs(x0), axis=(0,), keepdims=True) / 448.0).astype(np.float32)
    out = {}
    for k, v in d.items():
        if k == 'h':
            out['h_bytes'] = e4m3fn_bytes(x0 / s.astype(np.float64))
            out['h_scale'] = s
        else:
            out[k] = v
    return out


def reference(h_bytes, h_scale, adj, Qw_words, Qw_scales, Qb, Kw_words, Kw_scales, Kb):
    return core(e4m3fn_values(h_bytes) * h_scale.astype(np.float64), adj, Qw_words, Qw_scales, Qb, Kw_words, Kw_scales, Kb)

from contextlib import ExitStack

import concourse.mybir as mybir
from concourse.masks import make_identity

F32 = mybir.dt.float32
BF16 = mybir.dt.bfloat16
I32 = mybir.dt.int32
U32 = mybir.dt.uint32
U8 = mybir.dt.uint8
F8 = mybir.dt.float8_e4m3fn
X4 = mybir.dt.float8_e4m3fn_x4
ALU = mybir.AluOpType
ACT = mybir.ActivationFunctionType

P = 128
TOK = 2048
FEAT = 512
CH = 512
NCH = TOK // CH
NROW = TOK // P

FLOPS = 2 * TOK * FEAT * FEAT * 2 + 2 * TOK * TOK * FEAT

HALVES = (0, 1024), (1024, 2048)
NORM = [[(e, a, b) for a, b in HALVES] for e in "GGGSGGGSGGGSGSV"] + [[("V", 0, 512), ("S", 1536, 1920), ("V", 512, 1024), ("G", 1920, 2048), ("V", 1024, 1536)]]


def tile_gtransformerblock_pb_w8_kernel(tc, h_bytes, h_scale, adj, Qw_words, Qw_scales, Qb, Kw_words, Kw_scales, Kb, out):
    nc = tc.nc
    with ExitStack() as ctx:
        keep = ctx.enter_context(tc.tile_pool(name="keep", bufs=1))
        work = ctx.enter_context(tc.tile_pool(name="work", bufs=2))
        rows = ctx.enter_context(tc.tile_pool(name="rows", bufs=8))
        psum = ctx.enter_context(tc.psum_pool(name="psum", bufs=2))
        ctx.enter_context(tc.manual_schedule())

        hb = [keep.tile([P, 4 * FEAT], U8, name="hb%d" % c) for c in range(NCH)]

        def load_h(c):
            nc.sync.dma_start(out=hb[c][:], in_=h_bytes[c * CH : (c + 1) * CH, :].rearrange("(p r) k -> p (r k)", r=4))

        src = {"k": (Kw_words, Kw_scales, Kb), "q": (Qw_words, Qw_scales, Qb)}
        wraw, sraw, wcode, wplane, bias = {}, {}, {}, {}, {}
        warm = keep.tile([P, 1], F32, name="warm")
        nc.vector.memset(warm[:], 0.0)
        for nm in ("k", "q"):
            wraw[nm] = keep.tile([P, FEAT], I32, name="w_" + nm)
            sraw[nm] = keep.tile([P, FEAT], U8, name="s_" + nm)
            wcode[nm] = keep.tile([P, FEAT], I32, name="wp_" + nm, align_bytes=64)
            wplane[nm] = keep.tile([P, FEAT], U8, name="sp_" + nm, align_bytes=64)
            bias[nm] = keep.tile([P, 4], BF16, name="bias_" + nm)
            nc.vector.memset(sraw[nm][:].bitcast(I32), 0)

        hs4 = keep.tile([P, 4], F32, name="hs4")
        nc.scalar.dma_start(out=hs4[:], in_=h_scale.rearrange("o (p t) -> p (o t)", t=4))
        for nm in ("k", "q"):
            nc.scalar.dma_start(out=bias[nm][:], in_=src[nm][2].rearrange("(p t) -> p t", t=4))
        warm2 = keep.tile([P, 1], F32, name="warm2")
        nc.scalar.activation(out=warm2[:], in_=warm[:], func=ACT.Exp)

        ident = keep.tile([P, P], F32, name="ident")
        make_identity(nc, ident[:])
        hs8 = keep.tile([P, 2, 4], F32, name="hs8")
        nc.gpsimd.tensor_copy(out=hs8[:], in_=hs4[:].unsqueeze(1).to_broadcast([P, 2, 4]))

        def load_w(nm):
            words, scales = src[nm][:2]
            nc.sync.dma_start(out=wraw[nm][:], in_=words[0].rearrange("p n t -> p (n t)").bitcast(I32))
            for q in range(4):
                nc.sync.dma_start(out=sraw[nm][32 * q : 32 * q + 4, :].bitcast(I32), in_=scales[0, 4 * q : 4 * q + 4, :].bitcast(I32))

        def perm_w(nm):
            nc.vector.tensor_copy(out=wcode[nm][:].rearrange("p (t m) -> p t m", t=4), in_=wraw[nm][:].rearrange("p (m t) -> p t m", t=4))
            nc.vector.tensor_copy(out=wplane[nm][:].rearrange("p (t m) -> p t m", t=4), in_=sraw[nm][:].rearrange("p (m t) -> p t m", t=4))

        load_h(0)
        load_w("k")
        load_h(1)
        load_w("q")
        load_h(2)
        load_h(3)
        adj_t = []
        for i in range(NROW):
            t = rows.tile([P, TOK], BF16, tag="adj", name="adj%d" % i, bufs=12)
            nc.sync.dma_start(out=t[:], in_=adj[i * P : (i + 1) * P, :])
            adj_t.append(t)

        wide, ht, xts, hcode, hplane = {}, {}, {}, {}, {}
        for c in range(NCH):
            hcode[c] = keep.tile([P, CH], U32, name="hq%d" % c, align_bytes=64)
            hplane[c] = keep.tile([P, CH], U8, name="hp%d" % c, align_bytes=64)

        def h_begin(c):
            wide[c] = work.tile([P, 4 * FEAT], BF16, tag="wide", name="wide%d" % c, bufs=4)
            ht[c] = work.tile([P, CH * 4], BF16, tag="ht", name="ht%d" % c, align_bytes=64)

        def h_cast(eng, c, a, b):
            part = slice(a * FEAT, b * FEAT)
            dst, src8 = wide[c][:, part], hb[c][:, part].bitcast(F8)
            if eng == "S":
                nc.scalar.copy(out=dst, in_=src8)
            elif eng == "V":
                nc.vector.tensor_copy(out=dst, in_=src8)
            else:
                nc.gpsimd.tensor_copy(out=dst, in_=src8)

        def h_turn(c, b):
            xt = psum.tile([P, 4, P], F32, tag="bank", name="xt", bufs=8)
            words = wide[c][:].bitcast(F32)
            for x in range(4):
                r, u = 2 * b + x // 2, x % 2
                nc.tensor.transpose(xt[:, x, :], words[:, r * 256 + u : (r + 1) * 256 : 2], ident[:])
            xts[c, b] = xt

        def h_out_scaled(c, b):
            src4 = xts[c, b][:].rearrange("p x n -> p (x n)").bitcast(BF16).rearrange("p (x n e) -> p n x e", x=4, e=2)
            dst = ht[c][:].rearrange("p (n b x e) -> p b n x e", b=2, x=4, e=2)[:, b]
            sc = hs8[:].rearrange("p r t -> p (r t)").rearrange("p (x e) -> p x e", e=2).unsqueeze(1).to_broadcast([P, P, 4, 2])
            nc.vector.tensor_tensor(out=dst, in0=src4, in1=sc, op=ALU.mult)

        def h_quant(c):
            nc.vector.quantize_mx(out=hcode[c][:].bitcast(X4), scales=hplane[c][:], in_=ht[c][:])

        planes, grouped, code, plane = {}, {}, {}, {}

        def proj_begin(nm, c):
            planes[nm, c] = work.tile([P, 4, CH], BF16, tag="planes", name="planes_%s%d" % (nm, c), bufs=3)
            grouped[nm, c] = work.tile([P, CH, 4], BF16, tag="grouped", name="grouped_%s%d" % (nm, c), align_bytes=64, bufs=3)
            code[nm, c] = keep.tile([P, CH], U32, name="c_%s%d" % (nm, c), align_bytes=64)
            plane[nm, c] = keep.tile([P, CH], U8, name="p_%s%d" % (nm, c), align_bytes=64)

        def proj(nm, c, j):
            acc = psum.tile([P, CH], F32, tag="bank", name="acc", bufs=8)
            ch = slice(j * P, (j + 1) * P)
            nc.tensor.matmul_mx(out=acc[:], lhsT=wcode[nm][:, ch].bitcast(X4), lhsT_scale=wplane[nm][:, ch], rhs=hcode[c][:].bitcast(X4), rhs_scale=hplane[c][:], start=True, stop=True)
            nc.scalar.activation(out=planes[nm, c][:, j, :], in_=acc[:], func=ACT.Identity, bias=bias[nm][:, j : j + 1])

        def proj_all(nm, c, js=(0, 1, 2, 3)):
            if 0 in js:
                proj_begin(nm, c)
            for j in js:
                proj(nm, c, j)

        def direct(nm, c):
            grouped[nm, c] = work.tile([P, CH, 4], BF16, tag="grouped", name="grouped_%s%d" % (nm, c), align_bytes=64, bufs=3)
            code[nm, c] = keep.tile([P, CH], U32, name="c_%s%d" % (nm, c), align_bytes=64)
            plane[nm, c] = keep.tile([P, CH], U8, name="p_%s%d" % (nm, c), align_bytes=64)
            for g in range(4):
                acc = psum.tile([P, 4, P], F32, tag="bank", name="acc", bufs=8)
                cols = slice(g * P, (g + 1) * P)
                for j in range(4):
                    ch = slice(j * P, (j + 1) * P)
                    nc.tensor.matmul_mx(out=acc[:, j, :], lhsT=wcode[nm][:, ch].bitcast(X4), lhsT_scale=wplane[nm][:, ch], rhs=hcode[c][:, cols].bitcast(X4), rhs_scale=hplane[c][:, cols], start=True, stop=True)
                nc.vector.tensor_tensor(out=grouped[nm, c][:, cols, :], in0=acc[:].rearrange("p j n -> p n j"), in1=bias[nm][:].unsqueeze(1).to_broadcast([P, P, 4]), op=ALU.add)

        def group(eng, nm, c, a=0, b=CH):
            dst = grouped[nm, c][:, a:b, :]
            src4 = planes[nm, c][:, :, a:b].rearrange("p t n -> p n t")
            if eng == "S":
                nc.scalar.copy(out=dst, in_=src4)
            elif eng == "V":
                nc.vector.tensor_copy(out=dst, in_=src4)
            else:
                nc.gpsimd.tensor_scalar(out=dst, in0=src4, scalar1=1.0, scalar2=1.0, op0=ALU.mult, op1=ALU.mult)

        def proj_quant(nm, c):
            nc.vector.quantize_mx(out=code[nm, c][:].bitcast(X4), scales=plane[nm, c][:], in_=grouped[nm, c][:].rearrange("p n t -> p (n t)"))

        row, pair, negmax, total, recip = {}, {}, {}, {}, {}

        def block(i, c):
            if c == 0:
                row[i] = rows.tile([P, TOK], F32, tag="row", name="row%d" % i)
            sc = psum.tile([P, CH], F32, tag="bank", name="sc", bufs=8)
            g, rc = i // 4, slice((i % 4) * P, (i % 4 + 1) * P)
            nc.tensor.matmul_mx(out=sc[:], lhsT=code["q", g][:, rc].bitcast(X4), lhsT_scale=plane["q", g][:, rc], rhs=code["k", c][:].bitcast(X4), rhs_scale=plane["k", c][:], start=True, stop=True)
            cols = slice(c * CH, (c + 1) * CH)
            nc.vector.tensor_tensor(out=row[i][:, cols], in0=sc[:], in1=adj_t[i][:, cols], op=ALU.mult)

        def fold(i):
            pair[i] = work.tile([P, TOK // 2], BF16, tag="pair", name="pair%d" % i)
            nc.vector.tensor_tensor(out=pair[i][:], in0=row[i][:, : TOK // 2], in1=row[i][:, TOK // 2 :], op=ALU.max)

        def peak(i):
            junk = work.tile([P, TOK // 2], BF16, tag="junk", name="junk")
            negmax[i] = work.tile([P, 1], F32, tag="negmax", name="negmax%d" % i, bufs=6)
            nc.vector.tensor_scalar(out=junk[:], in0=pair[i][:], scalar1=-1.0, scalar2=None, op0=ALU.mult, op1=ALU.min, accum_out=negmax[i][:])

        def expo(i):
            total[i] = work.tile([P, 1], F32, tag="total", name="total%d" % i, bufs=6)
            nc.scalar.activation(out=row[i][:], in_=row[i][:], func=ACT.Exp, bias=negmax[i][:], accum_out=total[i][:])

        def norm(eng, i, a, b):
            r = row[i][:, a:b]
            if eng == "G":
                nc.gpsimd.tensor_scalar(out=r, in0=r, scalar1=recip[i][:], scalar2=1.0, op0=ALU.mult, op1=ALU.mult)
            elif eng == "S":
                nc.scalar.activation(out=r, in_=r, func=ACT.Copy, scale=recip[i][:])
            else:
                nc.vector.tensor_scalar(out=r, in0=r, scalar1=recip[i][:], scalar2=None, op0=ALU.mult)

        def store(i, a, b):
            nc.sync.dma_start(out=out[i * P : (i + 1) * P, a:b], in_=row[i][:, a:b])

        def inverse(i):
            recip[i] = work.tile([P, 1], F32, tag="recip", name="recip%d" % i, bufs=6)
            nc.vector.reciprocal(out=recip[i][:], in_=total[i][:])

        def finish(i):
            for eng, a, b in NORM[i]:
                norm(eng, i, a, b)
                store(i, a, b)

        for c in range(NCH):
            h_begin(c)
        h_cast("V", 0, 0, 2)
        h_cast("S", 0, 2, 4)
        h_turn(0, 0)
        h_turn(0, 1)
        h_cast("G", 1, 0, 2)
        h_cast("G", 1, 2, 4)
        h_cast("S", 2, 0, 2)
        h_cast("S", 2, 2, 4)
        h_cast("G", 3, 0, 2)
        h_cast("G", 3, 2, 4)
        perm_w("k")
        h_out_scaled(0, 0)
        h_out_scaled(0, 1)
        perm_w("q")
        for c in (1, 2):
            for b in range(2):
                h_turn(c, b)
        h_quant(0)
        proj_all("k", 0)
        group("G", "k", 0)
        h_out_scaled(1, 0)
        h_out_scaled(1, 1)
        h_out_scaled(2, 0)
        h_quant(1)
        h_out_scaled(2, 1)
        direct("q", 0)
        proj_all("k", 1)
        group("G", "k", 1)
        h_turn(3, 0)
        h_turn(3, 1)
        proj_quant("q", 0)
        h_out_scaled(3, 0)
        h_out_scaled(3, 1)
        proj_quant("k", 0)
        h_quant(2)
        proj_all("k", 2)
        group("S", "k", 2)
        h_quant(3)
        for c in range(NCH):
            for i in range(3):
                block(i, c)
                if c == 0 and i == 0:
                    proj_all("k", 3)
                    group("S", "k", 3, 0, 256)
                    group("G", "k", 3, 256, 512)
                if c == 3 and i > 0:
                    fold(i - 1)
            if c == 1:
                proj_all("q", 1)
                group("S", "q", 1)
            if c < 3:
                proj_quant("k", c + 1)
            else:
                peak(0)
                expo(0)
            block(3, c)
        peak(1)
        expo(1)
        fold(2)
        proj_quant("q", 1)
        peak(2)
        expo(2)
        for i in range(4, NROW):
            g = i // 4 + 1
            block(i, 0)
            block(i, 1)
            fold(i - 1)
            inverse(i - 4)
            finish(i - 4)
            block(i, 2)
            peak(i - 1)
            if i in (4, 8):
                proj_all("q", g, (0, 1))
            expo(i - 1)
            if i in (4, 8):
                proj_all("q", g, (2, 3))
            if i in (5, 9):
                group("S", "q", g)
            if i in (7, 11):
                proj_quant("q", g)
            block(i, 3)
        fold(NROW - 1)
        inverse(NROW - 4)
        finish(NROW - 4)
        peak(NROW - 1)
        expo(NROW - 1)
        for i in range(NROW - 3, NROW):
            inverse(i)
            finish(i)
